import numpy as np
import ml_dtypes


def mxq(x, axis, fmt="e4m3"):
    dtype, down = {"e4m3": (ml_dtypes.float8_e4m3fn, 7), "e5m2": (ml_dtypes.float8_e5m2, 14)}[fmt]
    v = np.moveaxis(np.asarray(x, np.float32).astype(ml_dtypes.bfloat16).astype(np.float64), axis, -1)
    blocks = v.reshape(v.shape[:-1] + (-1, 32))
    amax = np.abs(blocks).max(-1, keepdims=True)
    byte = np.maximum(np.where(amax > 0, np.frexp(amax)[1] - 1 + 127, 0) - down, 1)
    scale = np.exp2(byte - 127.0)
    codes = (blocks / scale).astype(np.float32).astype(dtype).astype(np.float64)
    return np.moveaxis((codes * scale).reshape(v.shape), -1, axis)


WIDE = False


def mx_kscale(k):
    if not WIDE:
        return np.ones(k)
    levels = np.array([10, -10, 5, -5, 0])
    if k % 512:
        return np.exp2(np.random.permutation(np.resize(levels, k // 32))).repeat(32)
    a = np.empty((k // 512, 16))
    for p in range(k // 512):
        a[p, :8] = np.random.permutation(np.resize(levels, 8))
        for g in range(8):
            far = levels[np.abs(levels - a[p, g]) >= 10]
            a[p, g + 8] = far[np.random.randint(len(far))]
    return np.exp2(a.ravel()).repeat(32)


BF16 = ml_dtypes.bfloat16


def bf(x):
    return np.asarray(x, np.float32).astype(BF16)


def f64(x):
    return np.asarray(x).astype(np.float64)


N, I0, O0, I1, O1, I2, O2, D0, D1, D2 = 4096, 512, 512, 128, 128, 128, 128, 1, 3, 5


def irrep_linear(x, w):
    return (x.transpose(2, 0, 1) @ w.transpose(2, 1, 0)).transpose(1, 2, 0)


def setup_inputs():
    s = mx_kscale(I0)
    return {"x0e": bf(np.random.standard_normal((N, I0, D0)) * s[None, :, None]),
            "x1o": bf(np.random.standard_normal((N, I1, D1))),
            "x2e": bf(np.random.standard_normal((N, I2, D2))),
            "w0e": bf(np.random.standard_normal((O0, I0, D0)) / np.sqrt(I0) / s[None, :, None]),
            "w1o": bf(np.random.standard_normal((O1, I1, D1)) / np.sqrt(I1)),
            "w2e": bf(np.random.standard_normal((O2, I2, D2)) / np.sqrt(I2)),
            "bias": bf(np.random.standard_normal(O0) * 0.5)}


def reference(x0e, x1o, x2e, w0e, w1o, w2e, bias):
    y0e = irrep_linear(mxq(f64(x0e), 1, "e4m3"), mxq(f64(w0e), 1, "e4m3")) + f64(bias)[None, :, None]
    y1o = irrep_linear(f64(x1o), f64(w1o))
    y2e = irrep_linear(f64(x2e), f64(w2e))
    n = x0e.shape[0]
    return np.concatenate([y0e.reshape(n, -1), y1o.reshape(n, -1), y2e.reshape(n, -1)], axis=-1)

@@ -1,0 +1,202 @@
+from contextlib import ExitStack
+
+import concourse.mybir as mybir
+from concourse.masks import make_identity
+
+F32 = mybir.dt.float32
+BF16 = mybir.dt.bfloat16
+U32 = mybir.dt.uint32
+U8 = mybir.dt.uint8
+FP8X4 = mybir.dt.float8_e4m3fn_x4
+ADD = mybir.AluOpType.add
+MULT = mybir.AluOpType.mult
+
+P = 128
+TOKENS = 4096
+TILES = TOKENS // P
+UNIT = 2
+UNITS = TILES // UNIT
+GROUP = 2
+K0 = 512
+O0 = 512
+COLS = 1536
+HALF = 64
+CHUNKS = (4, 4, 8, 16)
+
+FLOPS = 2 * TOKENS * (K0 * O0 + 3 * P * P + 5 * P * P)
+
+
+def tile_linearlayer_t_kernel(tc, x0e, x1o, x2e, w0e, w1o, w2e, bias, out):
+    nc = tc.nc
+    x0_rows = x0e.rearrange("(p t) i one -> p t (i one)", t=TILES)
+    x1_rows = x1o.rearrange("(p t) i m -> p t (i m)", t=TILES)
+    x2_rows = x2e.rearrange("(p t) i m -> p t (i m)", t=TILES)
+    out_rows = out.rearrange("(p t) c -> p t c", t=TILES)
+
+    with ExitStack() as ctx:
+        const = ctx.enter_context(tc.tile_pool(name="const", bufs=1))
+        xin = ctx.enter_context(tc.tile_pool(name="xin", bufs=1))
+        work = ctx.enter_context(tc.tile_pool(name="work", bufs=3))
+        split_pool = ctx.enter_context(tc.tile_pool(name="split_pool", bufs=4))
+        stage = ctx.enter_context(tc.tile_pool(name="stage", bufs=3))
+        psum = ctx.enter_context(tc.psum_pool(name="psum", bufs=8))
+        ctx.enter_context(tc.manual_schedule())
+
+        ident_b = const.tile([P, P], BF16)
+        make_identity(nc, ident_b[:])
+        ident_f = const.tile([P, P], F32)
+        make_identity(nc, ident_f[:])
+        bias_rows = const.tile([P, O0], BF16)
+        nc.vector.memset(bias_rows[:], 0.0)
+        ones = const.tile([P, P], BF16)
+        nc.vector.memset(ones[:], 1.0)
+
+        w1_sb = const.tile([P, 1, 3 * P], BF16)
+        nc.sync.dma_start(out=w1_sb[:], in_=w1o.rearrange("(n o) i m -> o n (i m)", n=1))
+        w2_sb = const.tile([P, 1, 5 * P], BF16)
+        nc.sync.dma_start(out=w2_sb[:], in_=w2e.rearrange("(n o) i m -> o n (i m)", n=1))
+        w0_sb = const.tile([P, 4, K0], BF16)
+
+        where = []
+        first = 0
+        for k, count in enumerate(CHUNKS):
+            x1c = xin.tile([P, count, 3 * P], BF16, name="x1c%d" % k)
+            nc.sync.dma_start(out=x1c[:], in_=x1_rows[:, first : first + count, :])
+            x2c = xin.tile([P, count, 5 * P], BF16, name="x2c%d" % k)
+            nc.sync.dma_start(out=x2c[:], in_=x2_rows[:, first : first + count, :])
+            if k == 0:
+                nc.sync.dma_start(out=w0_sb[:], in_=w0e.rearrange("(p t) i one -> p t (i one)", t=4))
+            x0c = xin.tile([P, count, K0], BF16, name="x0c%d" % k)
+            nc.sync.dma_start(out=x0c[:], in_=x0_rows[:, first : first + count, :])
+            if k == 0:
+                nc.sync.dma_start(out=bias_rows[0:1, :], in_=bias.rearrange("(r n) -> r n", r=1))
+            for j in range(count):
+                where.append((x0c, x1c, x2c, j))
+            first += count
+
+        def split_components(dst, src2):
+            nc.gpsimd.tensor_scalar(out=dst, in0=src2.rearrange("p (i m) -> p m i", m=5),
+                                    scalar1=1.0, scalar2=0.0, op0=MULT, op1=ADD)
+
+        def transpose_components(src1, src2):
+            bank_c = psum.tile([P, 8, P], BF16, tag="bank")
+            by_m = src1.rearrange("p (i m) -> p m i", m=3)
+            for c in range(3):
+                nc.tensor.transpose(bank_c[:, c, :], by_m[:, c, :], ident_b[:])
+            for c in range(5):
+                nc.tensor.transpose(bank_c[:, 3 + c, :], src2[:, c, :], ident_b[:])
+            return bank_c
+
+        def transpose_words(rows):
+            bank_w = psum.tile([P, 2, 2, P], F32, tag="bank")
+            for j in range(2):
+                words = rows[j].bitcast(F32)
+                for u in range(2):
+                    nc.tensor.transpose(bank_w[:, j, u, :], words[:, u : 2 * P : 2], ident_f[:])
+            return bank_w
+
+        w_split = const.tile([P, 5, P], BF16)
+        split_components(w_split[:], w2_sb[:, 0, :])
+        bank_wc = transpose_components(w1_sb[:, 0, :], w_split[:])
+        w_t = const.tile([P, 8, P], BF16)
+        nc.scalar.copy(out=w_t[:], in_=bank_wc[:])
+
+        w_grouped = const.tile([P, P, 4, 4], BF16, align_bytes=64)
+        for h in range(2):
+            bank_w0 = transpose_words([w0_sb[:, 2 * h, :], w0_sb[:, 2 * h + 1, :]])
+            nc.vector.tensor_copy(out=w_grouped[:, :, 2 * h : 2 * h + 2, :].bitcast(F32),
+                                  in_=bank_w0[:].rearrange("p j u r -> p r j u"))
+        w_codes = const.tile([P, O0], U32, align_bytes=64)
+        w_scales = const.tile([P, O0], U8, align_bytes=64)
+        nc.vector.quantize_mx(out=w_codes[:].bitcast(FP8X4), scales=w_scales[:],
+                              in_=w_grouped[:].rearrange("p r t v -> p (r t v)"))
+
+        bank_b = psum.tile([P, O0], F32, tag="bank")
+        nc.tensor.matmul(bank_b[:], lhsT=ones[:], rhs=bias_rows[:], start=True, stop=True)
+        bias_all = const.tile([P, O0], F32)
+        nc.scalar.copy(out=bias_all[:], in_=bank_b[:])
+
+        split_of = {}
+        xt_of = {}
+        grouped_of = {}
+        codes_of = {}
+        res_of = {}
+
+        def stage_a(s):
+            x0c, x1c, x2c, j = where[UNIT * s]
+            split = split_pool.tile([P, UNIT, 5, P], BF16)
+            for n in range(UNIT):
+                split_components(split[:, n], x2c[:, j + n, :])
+            split_of[s] = split
+
+        def stage_b(s):
+            x0c, x1c, x2c, j = where[UNIT * s]
+            split = split_of[s]
+            bank_w = transpose_words([x0c[:, j, :], x0c[:, j + 1, :]])
+            bank_c0 = transpose_components(x1c[:, j, :], split[:, 0])
+            bank_c1 = transpose_components(x1c[:, j + 1, :], split[:, 1])
+            grouped = work.tile([P, UNIT, P, 4], BF16, align_bytes=64)
+            nc.vector.tensor_copy(out=grouped[:].bitcast(F32), in_=bank_w[:].rearrange("p j u r -> p j r u"))
+            x_t = work.tile([P, UNIT, 8, P], BF16)
+            nc.scalar.copy(out=x_t[:, 0], in_=bank_c0[:])
+            nc.vector.tensor_copy(out=x_t[:, 1], in_=bank_c1[:])
+            xt_of[s] = x_t
+            grouped_of[s] = grouped
+
+        def quantise(s):
+            codes = work.tile([P, UNIT * P], U32, align_bytes=64)
+            scales = work.tile([P, UNIT * P], U8, align_bytes=64)
+            nc.vector.quantize_mx(out=codes[:].bitcast(FP8X4), scales=scales[:],
+                                  in_=grouped_of[s][:].rearrange("p j r t -> p (j r t)"))
+            codes_of[s] = (codes, scales)
+
+        def stage_c0(s):
+            codes, scales = codes_of[s]
+            if s % GROUP == 0:
+                res = stage.tile([P, GROUP * UNIT, COLS], F32)
+                res_of[s // GROUP] = res
+            res = res_of[s // GROUP]
+            base = (s % GROUP) * UNIT
+            accs = []
+            for j in range(UNIT):
+                acc = psum.tile([P, O0], F32, tag="bank")
+                cols = slice(j * P, (j + 1) * P)
+                nc.tensor.matmul_mx(out=acc[:], lhsT=codes[:, cols].bitcast(FP8X4), lhsT_scale=scales[:, cols],
+                                    rhs=w_codes[:].bitcast(FP8X4), rhs_scale=w_scales[:], start=True, stop=True)
+                accs.append(acc)
+            for j in range(UNIT):
+                nc.vector.tensor_tensor(out=res[:, base + j, 0:O0], in0=accs[j][:], in1=bias_all[:], op=ADD)
+
+        def stage_c1(s):
+            x_t = xt_of[s]
+            res = res_of[s // GROUP]
+            base = (s % GROUP) * UNIT
+            for j in range(UNIT):
+                y_1 = psum.tile([P, 3, P], F32, tag="bank")
+                for m in range(3):
+                    nc.tensor.matmul(y_1[:, m, :], lhsT=x_t[:, j, m, :], rhs=w_t[:, m, :], start=True, stop=True)
+                nc.scalar.copy(out=res[:, base + j, 512:896].rearrange("p (o m) -> p o m", m=3),
+                               in_=y_1[:].rearrange("p m o -> p o m"))
+                for h in range(2):
+                    y_2 = psum.tile([P, 5, HALF], F32, tag="bank")
+                    for m in range(5):
+                        nc.tensor.matmul(y_2[:, m, :], lhsT=x_t[:, j, 3 + m, :],
+                                         rhs=w_t[:, 3 + m, h * HALF : (h + 1) * HALF], start=True, stop=True)
+                    lo = 896 + 5 * HALF * h
+                    nc.scalar.copy(out=res[:, base + j, lo : lo + 5 * HALF].rearrange("p (o m) -> p o m", m=5),
+                                   in_=y_2[:].rearrange("p m o -> p o m"))
+            if s % GROUP == GROUP - 1:
+                t0 = UNIT * (s - GROUP + 1)
+                nc.sync.dma_start(out=out_rows[:, t0 : t0 + GROUP * UNIT, :], in_=res[:])
+
+        for s in range(-3, UNITS):
+            if s + 3 < UNITS:
+                stage_a(s + 3)
+            if 0 <= s + 1 < UNITS:
+                stage_b(s + 1)
+            if s >= 0:
+                stage_c0(s)
+            if 0 <= s + 1 < UNITS:
+                quantise(s + 1)
+            if s >= 0:
+                stage_c1(s)

@@ -129,19 +129,23 @@ def tile_linearlayer_t_kernel(tc, x0e, x1o, x2e, w0e, w1o, w2e, bias, out):
                 split_components(split[:, n], x2c[:, j + n, :])
             split_of[s] = split
 
-        def stage_b(s):
+        def words_of_x0(s):
             x0c, x1c, x2c, j = where[UNIT * s]
-            split = split_of[s]
             bank_w = transpose_words([x0c[:, j, :], x0c[:, j + 1, :]])
-            bank_c0 = transpose_components(x1c[:, j, :], split[:, 0])
-            bank_c1 = transpose_components(x1c[:, j + 1, :], split[:, 1])
             grouped = work.tile([P, UNIT, P, 4], BF16, align_bytes=64)
             nc.vector.tensor_copy(out=grouped[:].bitcast(F32), in_=bank_w[:].rearrange("p j u r -> p j r u"))
-            x_t = work.tile([P, UNIT, 8, P], BF16)
-            nc.scalar.copy(out=x_t[:, 0], in_=bank_c0[:])
-            nc.vector.tensor_copy(out=x_t[:, 1], in_=bank_c1[:])
-            xt_of[s] = x_t
             grouped_of[s] = grouped
+
+        def components(s, n):
+            x0c, x1c, x2c, j = where[UNIT * s]
+            if n == 0:
+                x_t = work.tile([P, UNIT, 8, P], BF16)
+                xt_of[s] = x_t
+            bank_c = transpose_components(x1c[:, j + n, :], split_of[s][:, n])
+            if n == 0:
+                nc.scalar.copy(out=xt_of[s][:, n], in_=bank_c[:])
+            else:
+                nc.vector.tensor_copy(out=xt_of[s][:, n], in_=bank_c[:])
 
         def quantise(s):
             codes = work.tile([P, UNIT * P], U32, align_bytes=64)
@@ -167,36 +171,43 @@ def tile_linearlayer_t_kernel(tc, x0e, x1o, x2e, w0e, w1o, w2e, bias, out):
             for j in range(UNIT):
                 nc.vector.tensor_tensor(out=res[:, base + j, 0:O0], in0=accs[j][:], in1=bias_all[:], op=ADD)
 
-        def stage_c1(s):
+        def plain(s, j):
             x_t = xt_of[s]
             res = res_of[s // GROUP]
             base = (s % GROUP) * UNIT
-            for j in range(UNIT):
-                y_1 = psum.tile([P, 3, P], F32, tag="bank")
-                for m in range(3):
-                    nc.tensor.matmul(y_1[:, m, :], lhsT=x_t[:, j, m, :], rhs=w_t[:, m, :], start=True, stop=True)
-                nc.scalar.copy(out=res[:, base + j, 512:896].rearrange("p (o m) -> p o m", m=3),
-                               in_=y_1[:].rearrange("p m o -> p o m"))
-                for h in range(2):
-                    y_2 = psum.tile([P, 5, HALF], F32, tag="bank")
-                    for m in range(5):
-                        nc.tensor.matmul(y_2[:, m, :], lhsT=x_t[:, j, 3 + m, :],
-                                         rhs=w_t[:, 3 + m, h * HALF : (h + 1) * HALF], start=True, stop=True)
-                    lo = 896 + 5 * HALF * h
-                    nc.scalar.copy(out=res[:, base + j, lo : lo + 5 * HALF].rearrange("p (o m) -> p o m", m=5),
-                                   in_=y_2[:].rearrange("p m o -> p o m"))
+            y_1 = psum.tile([P, 3, P], F32, tag="bank")
+            for m in range(3):
+                nc.tensor.matmul(y_1[:, m, :], lhsT=x_t[:, j, m, :], rhs=w_t[:, m, :], start=True, stop=True)
+            nc.scalar.copy(out=res[:, base + j, 512:896].rearrange("p (o m) -> p o m", m=3),
+                           in_=y_1[:].rearrange("p m o -> p o m"))
+            for h in range(2):
+                y_2 = psum.tile([P, 5, HALF], F32, tag="bank")
+                for m in range(5):
+                    nc.tensor.matmul(y_2[:, m, :], lhsT=x_t[:, j, 3 + m, :],
+                                     rhs=w_t[:, 3 + m, h * HALF : (h + 1) * HALF], start=True, stop=True)
+                lo = 896 + 5 * HALF * h
+                nc.scalar.copy(out=res[:, base + j, lo : lo + 5 * HALF].rearrange("p (o m) -> p o m", m=5),
+                               in_=y_2[:].rearrange("p m o -> p o m"))
+
+        def store(s):
             if s % GROUP == GROUP - 1:
                 t0 = UNIT * (s - GROUP + 1)
-                nc.sync.dma_start(out=out_rows[:, t0 : t0 + GROUP * UNIT, :], in_=res[:])
+                nc.sync.dma_start(out=out_rows[:, t0 : t0 + GROUP * UNIT, :], in_=res_of[s // GROUP][:])
 
         for s in range(-3, UNITS):
+            ahead = 0 <= s + 1 < UNITS
             if s + 3 < UNITS:
                 stage_a(s + 3)
-            if 0 <= s + 1 < UNITS:
-                stage_b(s + 1)
+            if ahead:
+                words_of_x0(s + 1)
             if s >= 0:
                 stage_c0(s)
-            if 0 <= s + 1 < UNITS:
+            if ahead:
                 quantise(s + 1)
+            for n in range(UNIT):
+                if s >= 0:
+                    plain(s, n)
+                if ahead:
+                    components(s + 1, n)
             if s >= 0:
-                stage_c1(s)
+                store(s)

@@ -87,6 +87,30 @@ def tile_linearlayer_t_kernel(tc, x0e, x1o, x2e, w0e, w1o, w2e, bias, out):
                 nc.tensor.transpose(bank_c[:, 3 + c, :], src2[:, c, :], ident_b[:])
             return bank_c
 
+        def pair_components(dst, src1, src2):
+            nc.gpsimd.tensor_scalar(out=dst[:, 0], in0=src1.rearrange("p (i m) -> p i m", m=3)[:, :, 0:2],
+                                    scalar1=1.0, scalar2=0.0, op0=MULT, op1=ADD)
+            by_m = src2.rearrange("p (i m) -> p i m", m=5)
+            for d in range(2):
+                nc.gpsimd.tensor_scalar(out=dst[:, 1 + d], in0=by_m[:, :, 2 * d : 2 * d + 2],
+                                        scalar1=1.0, scalar2=0.0, op0=MULT, op1=ADD)
+
+        def transpose_pairs(pairs, src1, src2):
+            bank_p = psum.tile([P, 4, P], F32, tag="bank")
+            for d in range(3):
+                nc.tensor.transpose(bank_p[:, d, :], pairs[:, d].rearrange("p i e -> p (i e)").bitcast(F32), ident_f[:])
+            last = bank_p[:, 3, :].bitcast(BF16)
+            nc.tensor.transpose(last[:, 0:P], src1.rearrange("p (i m) -> p i m", m=3)[:, :, 2], ident_b[:])
+            nc.tensor.transpose(last[:, P : 2 * P], src2.rearrange("p (i m) -> p i m", m=5)[:, :, 4], ident_b[:])
+            return bank_p
+
+        def component(x_t, j, c):
+            if c == 2 or c == 7:
+                h = c // 7
+                return x_t[:, j, 3, :].bitcast(BF16)[:, h * P : (h + 1) * P]
+            d, e = divmod(c if c < 2 else c - 1, 2)
+            return x_t[:, j, d, :].bitcast(BF16)[:, e : 2 * P : 2]
+
         def transpose_words(rows):
             bank_w = psum.tile([P, 2, 2, P], F32, tag="bank")
             for j in range(2):
@@ -124,9 +148,9 @@ def tile_linearlayer_t_kernel(tc, x0e, x1o, x2e, w0e, w1o, w2e, bias, out):
 
         def stage_a(s):
             x0c, x1c, x2c, j = where[UNIT * s]
-            split = split_pool.tile([P, UNIT, 5, P], BF16)
+            split = split_pool.tile([P, UNIT, 3, P, 2], BF16)
             for n in range(UNIT):
-                split_components(split[:, n], x2c[:, j + n, :])
+                pair_components(split[:, n], x1c[:, j + n, :], x2c[:, j + n, :])
             split_of[s] = split
 
         def words_of_x0(s):
@@ -139,9 +163,9 @@ def tile_linearlayer_t_kernel(tc, x0e, x1o, x2e, w0e, w1o, w2e, bias, out):
         def components(s, n):
             x0c, x1c, x2c, j = where[UNIT * s]
             if n == 0:
-                x_t = work.tile([P, UNIT, 8, P], BF16)
+                x_t = work.tile([P, UNIT, 4, P], F32)
                 xt_of[s] = x_t
-            bank_c = transpose_components(x1c[:, j + n, :], split_of[s][:, n])
+            bank_c = transpose_pairs(split_of[s][:, n], x1c[:, j + n, :], x2c[:, j + n, :])
             if n == 0:
                 nc.scalar.copy(out=xt_of[s][:, n], in_=bank_c[:])
             else:
@@ -177,13 +201,13 @@ def tile_linearlayer_t_kernel(tc, x0e, x1o, x2e, w0e, w1o, w2e, bias, out):
             base = (s % GROUP) * UNIT
             y_1 = psum.tile([P, 3, P], F32, tag="bank")
             for m in range(3):
-                nc.tensor.matmul(y_1[:, m, :], lhsT=x_t[:, j, m, :], rhs=w_t[:, m, :], start=True, stop=True)
+                nc.tensor.matmul(y_1[:, m, :], lhsT=component(x_t, j, m), rhs=w_t[:, m, :], start=True, stop=True)
             nc.scalar.copy(out=res[:, base + j, 512:896].rearrange("p (o m) -> p o m", m=3),
                            in_=y_1[:].rearrange("p m o -> p o m"))
             for h in range(2):
                 y_2 = psum.tile([P, 5, HALF], F32, tag="bank")
                 for m in range(5):
-                    nc.tensor.matmul(y_2[:, m, :], lhsT=x_t[:, j, 3 + m, :],
+                    nc.tensor.matmul(y_2[:, m, :], lhsT=component(x_t, j, 3 + m),
                                      rhs=w_t[:, 3 + m, h * HALF : (h + 1) * HALF], start=True, stop=True)
                 lo = 896 + 5 * HALF * h
                 nc.scalar.copy(out=res[:, base + j, lo : lo + 5 * HALF].rearrange("p (o m) -> p o m", m=5),

@@ -21,7 +21,8 @@ K0 = 512
 O0 = 512
 COLS = 1536
 HALF = 64
-CHUNKS = (4, 4, 8, 16)
+CHUNKS = (4, 8, 12, 8)
+EARLY = 3
 
 FLOPS = 2 * TOKENS * (K0 * O0 + 3 * P * P + 5 * P * P)
 
@@ -58,8 +59,9 @@ def tile_linearlayer_t_kernel(tc, x0e, x1o, x2e, w0e, w1o, w2e, bias, out):
         w0_sb = const.tile([P, 4, K0], BF16)
 
         where = []
-        first = 0
-        for k, count in enumerate(CHUNKS):
+
+        def load(k):
+            first, count = sum(CHUNKS[:k]), CHUNKS[k]
             x1c = xin.tile([P, count, 3 * P], BF16, name="x1c%d" % k)
             nc.sync.dma_start(out=x1c[:], in_=x1_rows[:, first : first + count, :])
             x2c = xin.tile([P, count, 5 * P], BF16, name="x2c%d" % k)
@@ -72,7 +74,9 @@ def tile_linearlayer_t_kernel(tc, x0e, x1o, x2e, w0e, w1o, w2e, bias, out):
                 nc.sync.dma_start(out=bias_rows[0:1, :], in_=bias.rearrange("(r n) -> r n", r=1))
             for j in range(count):
                 where.append((x0c, x1c, x2c, j))
-            first += count
+
+        for k in range(EARLY):
+            load(k)
 
         def split_components(dst, src2):
             nc.gpsimd.tensor_scalar(out=dst, in0=src2.rearrange("p (i m) -> p m i", m=5),
@@ -217,6 +221,9 @@ def tile_linearlayer_t_kernel(tc, x0e, x1o, x2e, w0e, w1o, w2e, bias, out):
             if s % GROUP == GROUP - 1:
                 t0 = UNIT * (s - GROUP + 1)
                 nc.sync.dma_start(out=out_rows[:, t0 : t0 + GROUP * UNIT, :], in_=res_of[s // GROUP][:])
+                k = EARLY + s // GROUP
+                if k < len(CHUNKS):
+                    load(k)
 
         for s in range(-3, UNITS):
             ahead = 0 <= s + 1 < UNITS

from contextlib import ExitStack

import concourse.mybir as mybir
from concourse.masks import make_identity

F32 = mybir.dt.float32
BF16 = mybir.dt.bfloat16
U32 = mybir.dt.uint32
U8 = mybir.dt.uint8
FP8X4 = mybir.dt.float8_e4m3fn_x4
ADD = mybir.AluOpType.add
MULT = mybir.AluOpType.mult

P = 128
TOKENS = 4096
TILES = TOKENS // P
UNIT = 2
UNITS = TILES // UNIT
GROUP = 2
K0 = 512
O0 = 512
COLS = 1536
HALF = 64
CHUNKS = (4, 8, 12, 8)
EARLY = 3

FLOPS = 2 * TOKENS * (K0 * O0 + 3 * P * P + 5 * P * P)


def tile_linearlayer_t_kernel(tc, x0e, x1o, x2e, w0e, w1o, w2e, bias, out):
    nc = tc.nc
    x0_rows = x0e.rearrange("(p t) i one -> p t (i one)", t=TILES)
    x1_rows = x1o.rearrange("(p t) i m -> p t (i m)", t=TILES)
    x2_rows = x2e.rearrange("(p t) i m -> p t (i m)", t=TILES)
    out_rows = out.rearrange("(p t) c -> p t c", t=TILES)

    with ExitStack() as ctx:
        const = ctx.enter_context(tc.tile_pool(name="const", bufs=1))
        xin = ctx.enter_context(tc.tile_pool(name="xin", bufs=1))
        work = ctx.enter_context(tc.tile_pool(name="work", bufs=3))
        split_pool = ctx.enter_context(tc.tile_pool(name="split_pool", bufs=4))
        stage = ctx.enter_context(tc.tile_pool(name="stage", bufs=3))
        psum = ctx.enter_context(tc.psum_pool(name="psum", bufs=8))
        ctx.enter_context(tc.manual_schedule())

        ident_b = const.tile([P, P], BF16)
        make_identity(nc, ident_b[:])
        ident_f = const.tile([P, P], F32)
        make_identity(nc, ident_f[:])
        bias_rows = const.tile([P, O0], BF16)
        nc.vector.memset(bias_rows[:], 0.0)
        ones = const.tile([P, P], BF16)
        nc.vector.memset(ones[:], 1.0)

        w1_sb = const.tile([P, 1, 3 * P], BF16)
        nc.sync.dma_start(out=w1_sb[:], in_=w1o.rearrange("(n o) i m -> o n (i m)", n=1))
        w2_sb = const.tile([P, 1, 5 * P], BF16)
        nc.sync.dma_start(out=w2_sb[:], in_=w2e.rearrange("(n o) i m -> o n (i m)", n=1))
        w0_sb = const.tile([P, 4, K0], BF16)

        where = []

        def load(k):
            first, count = sum(CHUNKS[:k]), CHUNKS[k]
            x1c = xin.tile([P, count, 3 * P], BF16, name="x1c%d" % k)
            nc.sync.dma_start(out=x1c[:], in_=x1_rows[:, first : first + count, :])
            x2c = xin.tile([P, count, 5 * P], BF16, name="x2c%d" % k)
            nc.sync.dma_start(out=x2c[:], in_=x2_rows[:, first : first + count, :])
            if k == 0:
                nc.sync.dma_start(out=w0_sb[:], in_=w0e.rearrange("(p t) i one -> p t (i one)", t=4))
            x0c = xin.tile([P, count, K0], BF16, name="x0c%d" % k)
            nc.sync.dma_start(out=x0c[:], in_=x0_rows[:, first : first + count, :])
            if k == 0:
                nc.sync.dma_start(out=bias_rows[0:1, :], in_=bias.rearrange("(r n) -> r n", r=1))
            for j in range(count):
                where.append((x0c, x1c, x2c, j))

        for k in range(EARLY):
            load(k)

        def split_components(dst, src2):
            nc.gpsimd.tensor_scalar(out=dst, in0=src2.rearrange("p (i m) -> p m i", m=5),
                                    scalar1=1.0, scalar2=0.0, op0=MULT, op1=ADD)

        def transpose_components(src1, src2):
            bank_c = psum.tile([P, 8, P], BF16, tag="bank")
            by_m = src1.rearrange("p (i m) -> p m i", m=3)
            for c in range(3):
                nc.tensor.transpose(bank_c[:, c, :], by_m[:, c, :], ident_b[:])
            for c in range(5):
                nc.tensor.transpose(bank_c[:, 3 + c, :], src2[:, c, :], ident_b[:])
            return bank_c

        def pair_components(dst, src1, src2):
            nc.gpsimd.tensor_scalar(out=dst[:, 0], in0=src1.rearrange("p (i m) -> p i m", m=3)[:, :, 0:2],
                                    scalar1=1.0, scalar2=0.0, op0=MULT, op1=ADD)
            by_m = src2.rearrange("p (i m) -> p i m", m=5)
            for d in range(2):
                nc.gpsimd.tensor_scalar(out=dst[:, 1 + d], in0=by_m[:, :, 2 * d : 2 * d + 2],
                                        scalar1=1.0, scalar2=0.0, op0=MULT, op1=ADD)

        def transpose_pairs(pairs, src1, src2):
            bank_p = psum.tile([P, 4, P], F32, tag="bank")
            for d in range(3):
                nc.tensor.transpose(bank_p[:, d, :], pairs[:, d].rearrange("p i e -> p (i e)").bitcast(F32), ident_f[:])
            last = bank_p[:, 3, :].bitcast(BF16)
            nc.tensor.transpose(last[:, 0:P], src1.rearrange("p (i m) -> p i m", m=3)[:, :, 2], ident_b[:])
            nc.tensor.transpose(last[:, P : 2 * P], src2.rearrange("p (i m) -> p i m", m=5)[:, :, 4], ident_b[:])
            return bank_p

        def component(x_t, j, c):
            if c == 2 or c == 7:
                h = c // 7
                return x_t[:, j, 3, :].bitcast(BF16)[:, h * P : (h + 1) * P]
            d, e = divmod(c if c < 2 else c - 1, 2)
            return x_t[:, j, d, :].bitcast(BF16)[:, e : 2 * P : 2]

        def transpose_words(rows):
            bank_w = psum.tile([P, 2, 2, P], F32, tag="bank")
            for j in range(2):
                words = rows[j].bitcast(F32)
                for u in range(2):
                    nc.tensor.transpose(bank_w[:, j, u, :], words[:, u : 2 * P : 2], ident_f[:])
            return bank_w

        w_split = const.tile([P, 5, P], BF16)
        split_components(w_split[:], w2_sb[:, 0, :])
        bank_wc = transpose_components(w1_sb[:, 0, :], w_split[:])
        w_t = const.tile([P, 8, P], BF16)
        nc.scalar.copy(out=w_t[:], in_=bank_wc[:])

        w_grouped = const.tile([P, P, 4, 4], BF16, align_bytes=64)
        for h in range(2):
            bank_w0 = transpose_words([w0_sb[:, 2 * h, :], w0_sb[:, 2 * h + 1, :]])
            nc.vector.tensor_copy(out=w_grouped[:, :, 2 * h : 2 * h + 2, :].bitcast(F32),
                                  in_=bank_w0[:].rearrange("p j u r -> p r j u"))
        w_codes = const.tile([P, O0], U32, align_bytes=64)
        w_scales = const.tile([P, O0], U8, align_bytes=64)
        nc.vector.quantize_mx(out=w_codes[:].bitcast(FP8X4), scales=w_scales[:],
                              in_=w_grouped[:].rearrange("p r t v -> p (r t v)"))

        bank_b = psum.tile([P, O0], F32, tag="bank")
        nc.tensor.matmul(bank_b[:], lhsT=ones[:], rhs=bias_rows[:], start=True, stop=True)
        bias_all = const.tile([P, O0], F32)
        nc.scalar.copy(out=bias_all[:], in_=bank_b[:])

        split_of = {}
        xt_of = {}
        grouped_of = {}
        codes_of = {}
        res_of = {}

        def stage_a(s):
            x0c, x1c, x2c, j = where[UNIT * s]
            split = split_pool.tile([P, UNIT, 3, P, 2], BF16)
            for n in range(UNIT):
                pair_components(split[:, n], x1c[:, j + n, :], x2c[:, j + n, :])
            split_of[s] = split

        def words_of_x0(s):
            x0c, x1c, x2c, j = where[UNIT * s]
            bank_w = transpose_words([x0c[:, j, :], x0c[:, j + 1, :]])
            grouped = work.tile([P, UNIT, P, 4], BF16, align_bytes=64)
            nc.vector.tensor_copy(out=grouped[:].bitcast(F32), in_=bank_w[:].rearrange("p j u r -> p j r u"))
            grouped_of[s] = grouped

        def components(s, n):
            x0c, x1c, x2c, j = where[UNIT * s]
            if n == 0:
                x_t = work.tile([P, UNIT, 4, P], F32)
                xt_of[s] = x_t
            bank_c = transpose_pairs(split_of[s][:, n], x1c[:, j + n, :], x2c[:, j + n, :])
            if n == 0:
                nc.scalar.copy(out=xt_of[s][:, n], in_=bank_c[:])
            else:
                nc.vector.tensor_copy(out=xt_of[s][:, n], in_=bank_c[:])

        def quantise(s):
            codes = work.tile([P, UNIT * P], U32, align_bytes=64)
            scales = work.tile([P, UNIT * P], U8, align_bytes=64)
            nc.vector.quantize_mx(out=codes[:].bitcast(FP8X4), scales=scales[:],
                                  in_=grouped_of[s][:].rearrange("p j r t -> p (j r t)"))
            codes_of[s] = (codes, scales)

        def stage_c0(s):
            codes, scales = codes_of[s]
            if s % GROUP == 0:
                res = stage.tile([P, GROUP * UNIT, COLS], F32)
                res_of[s // GROUP] = res
            res = res_of[s // GROUP]
            base = (s % GROUP) * UNIT
            accs = []
            for j in range(UNIT):
                acc = psum.tile([P, O0], F32, tag="bank")
                cols = slice(j * P, (j + 1) * P)
                nc.tensor.matmul_mx(out=acc[:], lhsT=codes[:, cols].bitcast(FP8X4), lhsT_scale=scales[:, cols],
                                    rhs=w_codes[:].bitcast(FP8X4), rhs_scale=w_scales[:], start=True, stop=True)
                accs.append(acc)
            for j in range(UNIT):
                nc.vector.tensor_tensor(out=res[:, base + j, 0:O0], in0=accs[j][:], in1=bias_all[:], op=ADD)

        def plain(s, j):
            x_t = xt_of[s]
            res = res_of[s // GROUP]
            base = (s % GROUP) * UNIT
            y_1 = psum.tile([P, 3, P], F32, tag="bank")
            for m in range(3):
                nc.tensor.matmul(y_1[:, m, :], lhsT=component(x_t, j, m), rhs=w_t[:, m, :], start=True, stop=True)
            nc.scalar.copy(out=res[:, base + j, 512:896].rearrange("p (o m) -> p o m", m=3),
                           in_=y_1[:].rearrange("p m o -> p o m"))
            for h in range(2):
                y_2 = psum.tile([P, 5, HALF], F32, tag="bank")
                for m in range(5):
                    nc.tensor.matmul(y_2[:, m, :], lhsT=component(x_t, j, 3 + m),
                                     rhs=w_t[:, 3 + m, h * HALF : (h + 1) * HALF], start=True, stop=True)
                lo = 896 + 5 * HALF * h
                nc.scalar.copy(out=res[:, base + j, lo : lo + 5 * HALF].rearrange("p (o m) -> p o m", m=5),
                               in_=y_2[:].rearrange("p m o -> p o m"))

        def store(s):
            if s % GROUP == GROUP - 1:
                t0 = UNIT * (s - GROUP + 1)
                nc.sync.dma_start(out=out_rows[:, t0 : t0 + GROUP * UNIT, :], in_=res_of[s // GROUP][:])
                k = EARLY + s // GROUP
                if k < len(CHUNKS):
                    load(k)

        for s in range(-3, UNITS):
            ahead = 0 <= s + 1 < UNITS
            if s + 3 < UNITS:
                stage_a(s + 3)
            if ahead:
                words_of_x0(s + 1)
            if s >= 0:
                stage_c0(s)
            if ahead:
                quantise(s + 1)
            for n in range(UNIT):
                if s >= 0:
                    plain(s, n)
                if ahead:
                    components(s + 1, n)
            if s >= 0:
                store(s)
